import numpy as np
import ml_dtypes

BF16 = ml_dtypes.bfloat16


def bf(x):
    return np.asarray(x, np.float32).astype(BF16)


def f32(x):
    return np.asarray(x, np.float32)


def f64(x):
    return np.asarray(x).astype(np.float64)


def striped(idx):
    return np.tile(idx.reshape(-1, 16).T, (8, 1))


F, K, C, S, N = 128, 128, 512, 2048, 256
OMEGA0, SCALE0 = 30.0, 5.0
W1, W2, B1, B2 = 0.01, 0.06, 0.04, 0.1


def setup_inputs():
    wcol = np.repeat(np.array([W1, W1, W2, W2]), F)
    brow = np.repeat(np.array([B1, B1, B2, B2]), F)
    bias = f32(np.random.uniform(-1.0, 1.0, (C, S)) * brow[:, None])
    w = bf(np.random.standard_normal((K, C)) * wcol[None, :] / np.sqrt(K))
    x = bf(np.random.standard_normal((K, N)))
    return {"bias": bias, "w": w, "x": x, "offs": striped(np.random.permutation(np.tile(np.arange(S), 2))[:N])}


def reference(bias, w, x, offs):
    idx = offs[:16].T.reshape(-1)
    lin = f64(w).T @ f64(x) + f64(bias)[:, idx]
    re1, im1, re2, im2 = lin.reshape(C // F, F, N)
    amp = np.exp(-OMEGA0 * im1 - SCALE0 * SCALE0 * (re1 * re1 + im1 * im1 + re2 * re2 + im2 * im2))
    return np.concatenate([amp * np.cos(OMEGA0 * re1), amp * np.sin(OMEGA0 * re1)], axis=0)

@@ -1,0 +1,86 @@
+import math
+
+import concourse.mybir as mybir
+
+F32 = mybir.dt.float32
+BF16 = mybir.dt.bfloat16
+U16 = mybir.dt.uint16
+I32 = mybir.dt.int32
+ALU = mybir.AluOpType
+FUNC = mybir.ActivationFunctionType
+
+P = 128
+N = 256
+S = 2048
+BLOCKS = 4
+
+FLOPS = 2 * P * (BLOCKS * P) * N
+
+OMEGA = 30.0
+DECAY = 25.0
+TURNS = OMEGA / (2.0 * math.pi)
+RADIANS = 6.283185
+
+
+def tile_adaptivemultigabor2dlayer_kernel(tc, bias, w, x, offs, out):
+    nc = tc.nc
+    with (
+        tc.tile_pool(name="held", bufs=1) as held,
+        tc.psum_pool(name="psum", bufs=1) as psum,
+    ):
+        offsets = held.tile([P, N // 16], U16, name="offsets")
+        nc.sync.dma_start(offsets[:], offs)
+        x_sb = held.tile([P, N], BF16, name="x_sb")
+        nc.sync.dma_start(x_sb[:], x)
+        w_sb = held.tile([P, BLOCKS * P], BF16, name="w_sb")
+        nc.sync.dma_start(w_sb[:], w)
+        windows = []
+        for b in range(BLOCKS):
+            window = held.tile([P, S], F32, name=f"window{b}")
+            nc.sync.dma_start(window[:], bias[b * P : (b + 1) * P, :])
+            windows.append(window)
+
+        projections = []
+        for b in range(BLOCKS):
+            bank = psum.tile([P, N], F32, name=f"bank{b}")
+            nc.tensor.matmul(bank[:], w_sb[:, b * P : (b + 1) * P], x_sb[:], start=True, stop=True)
+            proj = held.tile([P, N], F32, name=f"proj{b}")
+            nc.scalar.copy(proj[:], bank[:])
+            projections.append(proj)
+
+        lin = []
+        for b in range(BLOCKS):
+            lin_b = held.tile([P, N], F32, name=f"lin{b}")
+            nc.vector.tensor_tensor(lin_b[:], windows[b][:].indirect(offsets[:]), projections[b][:], ALU.add)
+            lin.append(lin_b)
+        re1, im1, re2, im2 = lin
+
+        whole = held.tile([P, N], I32, name="whole")
+        nc.vector.tensor_scalar(whole[:], re1[:], TURNS, None, ALU.mult)
+        part = held.tile([P, N], F32, name="part")
+        nc.vector.scalar_tensor_tensor(part[:], re1[:], TURNS, whole[:], ALU.mult, ALU.subtract)
+        flipped = held.tile([P, N], F32, name="flipped")
+        nc.vector.scalar_tensor_tensor(flipped[:], part[:], 0.5, part[:], ALU.is_gt, ALU.subtract)
+        angle = held.tile([P, 2, N], F32, name="angle")
+        nc.vector.scalar_tensor_tensor(angle[:, 1, :], flipped[:], 0.5, flipped[:], ALU.is_gt, ALU.subtract)
+        minus_abs = held.tile([P, N], F32, name="minus_abs")
+        nc.vector.scalar_tensor_tensor(minus_abs[:], angle[:, 1, :], -1.0, angle[:, 1, :], ALU.mult, ALU.min)
+        nc.vector.tensor_scalar(angle[:, 0, :], minus_abs[:], 0.25, None, ALU.add)
+        trig = held.tile([P, 2, N], F32, name="trig")
+        nc.scalar.activation(trig[:], angle[:], FUNC.Sin, scale=RADIANS)
+
+        total = held.tile([P, N], F32, name="total")
+        nc.vector.tensor_tensor(total[:], re1[:], re1[:], ALU.mult)
+        term = held.tile([P, N], F32, name="term_im1")
+        nc.vector.scalar_tensor_tensor(term[:], im1[:], OMEGA / DECAY, im1[:], ALU.add, ALU.mult)
+        nc.vector.tensor_tensor(total[:], total[:], term[:], ALU.add)
+        for name, block in (("re2", re2), ("im2", im2)):
+            square = held.tile([P, N], F32, name=f"square_{name}")
+            nc.vector.tensor_tensor(square[:], block[:], block[:], ALU.mult)
+            nc.vector.tensor_tensor(total[:], total[:], square[:], ALU.add)
+        amp = held.tile([P, N], F32, name="amp")
+        nc.scalar.activation(amp[:], total[:], FUNC.Exp, scale=-DECAY)
+
+        result = held.tile([P, 2, N], F32, name="result")
+        nc.vector.tensor_tensor(result[:], trig[:], amp[:].unsqueeze(1).to_broadcast([P, 2, N]), ALU.mult)
+        nc.sync.dma_start(out.rearrange("(h p) j -> p h j", p=P), result[:])

@@ -48,12 +48,12 @@ def tile_adaptivemultigabor2dlayer_kernel(tc, bias, w, x, offs, out):
             nc.scalar.copy(proj[:], bank[:])
             projections.append(proj)
 
-        lin = []
-        for b in range(BLOCKS):
-            lin_b = held.tile([P, N], F32, name=f"lin{b}")
-            nc.vector.tensor_tensor(lin_b[:], windows[b][:].indirect(offsets[:]), projections[b][:], ALU.add)
-            lin.append(lin_b)
-        re1, im1, re2, im2 = lin
+        def looked_up_plus_projection(b):
+            lin = held.tile([P, N], F32, name=f"lin{b}")
+            nc.vector.tensor_tensor(lin[:], windows[b][:].indirect(offsets[:]), projections[b][:], ALU.add)
+            return lin
+
+        re1 = looked_up_plus_projection(0)
 
         whole = held.tile([P, N], I32, name="whole")
         nc.vector.tensor_scalar(whole[:], re1[:], TURNS, None, ALU.mult)
@@ -69,18 +69,22 @@ def tile_adaptivemultigabor2dlayer_kernel(tc, bias, w, x, offs, out):
         trig = held.tile([P, 2, N], F32, name="trig")
         nc.scalar.activation(trig[:], angle[:], FUNC.Sin, scale=RADIANS)
 
-        total = held.tile([P, N], F32, name="total")
-        nc.vector.tensor_tensor(total[:], re1[:], re1[:], ALU.mult)
-        term = held.tile([P, N], F32, name="term_im1")
+        first = held.tile([P, N], F32, name="first")
+        nc.vector.tensor_tensor(first[:], re1[:], re1[:], ALU.mult)
+        im1 = looked_up_plus_projection(1)
+        term = held.tile([P, N], F32, name="term")
         nc.vector.scalar_tensor_tensor(term[:], im1[:], OMEGA / DECAY, im1[:], ALU.add, ALU.mult)
-        nc.vector.tensor_tensor(total[:], total[:], term[:], ALU.add)
-        for name, block in (("re2", re2), ("im2", im2)):
-            square = held.tile([P, N], F32, name=f"square_{name}")
-            nc.vector.tensor_tensor(square[:], block[:], block[:], ALU.mult)
-            nc.vector.tensor_tensor(total[:], total[:], square[:], ALU.add)
-        amp = held.tile([P, N], F32, name="amp")
-        nc.scalar.activation(amp[:], total[:], FUNC.Exp, scale=-DECAY)
+        nc.vector.tensor_tensor(first[:], first[:], term[:], ALU.add)
+        factor = held.tile([P, N], F32, name="factor_first")
+        nc.scalar.activation(factor[:], first[:], FUNC.Exp, scale=-DECAY)
 
         result = held.tile([P, 2, N], F32, name="result")
-        nc.vector.tensor_tensor(result[:], trig[:], amp[:].unsqueeze(1).to_broadcast([P, 2, N]), ALU.mult)
+        nc.vector.tensor_tensor(result[:], trig[:], factor[:].unsqueeze(1).to_broadcast([P, 2, N]), ALU.mult)
+        for b in (2, 3):
+            lin = looked_up_plus_projection(b)
+            square = held.tile([P, N], F32, name=f"square{b}")
+            nc.vector.tensor_tensor(square[:], lin[:], lin[:], ALU.mult)
+            factor = held.tile([P, N], F32, name=f"factor{b}")
+            nc.scalar.activation(factor[:], square[:], FUNC.Exp, scale=-DECAY)
+            nc.vector.tensor_tensor(result[:], result[:], factor[:].unsqueeze(1).to_broadcast([P, 2, N]), ALU.mult)
         nc.sync.dma_start(out.rearrange("(h p) j -> p h j", p=P), result[:])

@@ -13,13 +13,15 @@ P = 128
 N = 256
 S = 2048
 BLOCKS = 4
+PIECES = 2
+PIECE = N // PIECES
 
 FLOPS = 2 * P * (BLOCKS * P) * N
 
 OMEGA = 30.0
 DECAY = 25.0
 TURNS = OMEGA / (2.0 * math.pi)
-RADIANS = 6.283185
+PI_INSIDE = 3.1415925
 
 
 def tile_adaptivemultigabor2dlayer_kernel(tc, bias, w, x, offs, out):
@@ -39,13 +41,15 @@ def tile_adaptivemultigabor2dlayer_kernel(tc, bias, w, x, offs, out):
             window = held.tile([P, S], F32, name=f"window{b}")
             nc.sync.dma_start(window[:], bias[b * P : (b + 1) * P, :])
             windows.append(window)
+        quarter_turn = held.tile([P, 1], F32, name="quarter_turn")
+        nc.gpsimd.memset(quarter_turn[:], math.pi / 2.0)
 
         projections = []
         for b in range(BLOCKS):
             bank = psum.tile([P, N], F32, name=f"bank{b}")
             nc.tensor.matmul(bank[:], w_sb[:, b * P : (b + 1) * P], x_sb[:], start=True, stop=True)
             proj = held.tile([P, N], F32, name=f"proj{b}")
-            nc.scalar.copy(proj[:], bank[:])
+            nc.vector.tensor_copy(proj[:], bank[:])
             projections.append(proj)
 
         def looked_up_plus_projection(b):
@@ -53,38 +57,64 @@ def tile_adaptivemultigabor2dlayer_kernel(tc, bias, w, x, offs, out):
             nc.vector.tensor_tensor(lin[:], windows[b][:].indirect(offsets[:]), projections[b][:], ALU.add)
             return lin
 
-        re1 = looked_up_plus_projection(0)
+        def piece_looked_up_plus_projection(b, piece):
+            lin = held.tile([P, PIECE], F32, name=f"lin{b}_{piece}")
+            nc.vector.tensor_tensor(
+                lin[:],
+                windows[b][:].indirect(offsets[:, piece * (PIECE // 16) : (piece + 1) * (PIECE // 16)]),
+                projections[b][:, piece * PIECE : (piece + 1) * PIECE],
+                ALU.add,
+            )
+            return lin
 
+        re1 = looked_up_plus_projection(0)
         whole = held.tile([P, N], I32, name="whole")
         nc.vector.tensor_scalar(whole[:], re1[:], TURNS, None, ALU.mult)
+        total = held.tile([P, N], F32, name="total")
+        nc.vector.tensor_tensor(total[:], re1[:], re1[:], ALU.mult)
         part = held.tile([P, N], F32, name="part")
         nc.vector.scalar_tensor_tensor(part[:], re1[:], TURNS, whole[:], ALU.mult, ALU.subtract)
-        flipped = held.tile([P, N], F32, name="flipped")
-        nc.vector.scalar_tensor_tensor(flipped[:], part[:], 0.5, part[:], ALU.is_gt, ALU.subtract)
-        angle = held.tile([P, 2, N], F32, name="angle")
-        nc.vector.scalar_tensor_tensor(angle[:, 1, :], flipped[:], 0.5, flipped[:], ALU.is_gt, ALU.subtract)
+        sin_half = held.tile([P, N], F32, name="sin_half")
+        nc.scalar.activation(sin_half[:], part[:], FUNC.Sin, scale=PI_INSIDE)
         minus_abs = held.tile([P, N], F32, name="minus_abs")
-        nc.vector.scalar_tensor_tensor(minus_abs[:], angle[:, 1, :], -1.0, angle[:, 1, :], ALU.mult, ALU.min)
-        nc.vector.tensor_scalar(angle[:, 0, :], minus_abs[:], 0.25, None, ALU.add)
-        trig = held.tile([P, 2, N], F32, name="trig")
-        nc.scalar.activation(trig[:], angle[:], FUNC.Sin, scale=RADIANS)
+        nc.vector.scalar_tensor_tensor(minus_abs[:], part[:], -1.0, part[:], ALU.mult, ALU.min)
+        cos_half = held.tile([P, N], F32, name="cos_half")
+        nc.scalar.activation(cos_half[:], minus_abs[:], FUNC.Sin, bias=quarter_turn[:], scale=PI_INSIDE)
 
-        first = held.tile([P, N], F32, name="first")
-        nc.vector.tensor_tensor(first[:], re1[:], re1[:], ALU.mult)
         im1 = looked_up_plus_projection(1)
+        cos_less_1 = held.tile([P, N], F32, name="cos_less_1")
+        nc.vector.scalar_tensor_tensor(cos_less_1[:], sin_half[:], -2.0, sin_half[:], ALU.mult, ALU.mult)
         term = held.tile([P, N], F32, name="term")
         nc.vector.scalar_tensor_tensor(term[:], im1[:], OMEGA / DECAY, im1[:], ALU.add, ALU.mult)
-        nc.vector.tensor_tensor(first[:], first[:], term[:], ALU.add)
-        factor = held.tile([P, N], F32, name="factor_first")
-        nc.scalar.activation(factor[:], first[:], FUNC.Exp, scale=-DECAY)
+        sin_full = held.tile([P, N], F32, name="sin_full")
+        nc.vector.scalar_tensor_tensor(sin_full[:], sin_half[:], 2.0, cos_half[:], ALU.mult, ALU.mult)
+        nc.vector.tensor_tensor(total[:], total[:], term[:], ALU.add)
 
+        re2 = looked_up_plus_projection(2)
+        square = held.tile([P, N], F32, name="square_re2")
+        nc.vector.tensor_tensor(square[:], re2[:], re2[:], ALU.mult)
+        nc.vector.tensor_tensor(total[:], total[:], square[:], ALU.add)
+        factor = held.tile([P, N], F32, name="factor")
+        nc.scalar.activation(factor[:], total[:], FUNC.Exp, scale=-DECAY)
+
+        im2 = [piece_looked_up_plus_projection(3, piece) for piece in range(PIECES)]
+        last_factor = []
+        for piece in range(PIECES):
+            square = held.tile([P, PIECE], F32, name=f"square_im2_{piece}")
+            nc.vector.tensor_tensor(square[:], im2[piece][:], im2[piece][:], ALU.mult)
+            last = held.tile([P, PIECE], F32, name=f"last_factor{piece}")
+            nc.scalar.activation(last[:], square[:], FUNC.Exp, scale=-DECAY)
+            last_factor.append(last)
         result = held.tile([P, 2, N], F32, name="result")
-        nc.vector.tensor_tensor(result[:], trig[:], factor[:].unsqueeze(1).to_broadcast([P, 2, N]), ALU.mult)
-        for b in (2, 3):
-            lin = looked_up_plus_projection(b)
-            square = held.tile([P, N], F32, name=f"square{b}")
-            nc.vector.tensor_tensor(square[:], lin[:], lin[:], ALU.mult)
-            factor = held.tile([P, N], F32, name=f"factor{b}")
-            nc.scalar.activation(factor[:], square[:], FUNC.Exp, scale=-DECAY)
-            nc.vector.tensor_tensor(result[:], result[:], factor[:].unsqueeze(1).to_broadcast([P, 2, N]), ALU.mult)
-        nc.sync.dma_start(out.rearrange("(h p) j -> p h j", p=P), result[:])
+        nc.vector.scalar_tensor_tensor(result[:, 0, :], cos_less_1[:], 1.0, factor[:], ALU.add, ALU.mult)
+        nc.vector.tensor_tensor(result[:, 1, :], sin_full[:], factor[:], ALU.mult)
+        out_halves = out.rearrange("(h p) j -> p h j", p=P)
+        for piece in range(PIECES):
+            columns = slice(piece * PIECE, (piece + 1) * PIECE)
+            nc.vector.tensor_tensor(
+                result[:, :, columns],
+                result[:, :, columns],
+                last_factor[piece][:].unsqueeze(1).to_broadcast([P, 2, PIECE]),
+                ALU.mult,
+            )
+            nc.sync.dma_start(out_halves[:, :, columns], result[:, :, columns])

@@ -13,8 +13,6 @@ P = 128
 N = 256
 S = 2048
 BLOCKS = 4
-PIECES = 2
-PIECE = N // PIECES
 
 FLOPS = 2 * P * (BLOCKS * P) * N
 
@@ -57,16 +55,6 @@ def tile_adaptivemultigabor2dlayer_kernel(tc, bias, w, x, offs, out):
             nc.vector.tensor_tensor(lin[:], windows[b][:].indirect(offsets[:]), projections[b][:], ALU.add)
             return lin
 
-        def piece_looked_up_plus_projection(b, piece):
-            lin = held.tile([P, PIECE], F32, name=f"lin{b}_{piece}")
-            nc.vector.tensor_tensor(
-                lin[:],
-                windows[b][:].indirect(offsets[:, piece * (PIECE // 16) : (piece + 1) * (PIECE // 16)]),
-                projections[b][:, piece * PIECE : (piece + 1) * PIECE],
-                ALU.add,
-            )
-            return lin
-
         re1 = looked_up_plus_projection(0)
         whole = held.tile([P, N], I32, name="whole")
         nc.vector.tensor_scalar(whole[:], re1[:], TURNS, None, ALU.mult)
@@ -97,24 +85,15 @@ def tile_adaptivemultigabor2dlayer_kernel(tc, bias, w, x, offs, out):
         factor = held.tile([P, N], F32, name="factor")
         nc.scalar.activation(factor[:], total[:], FUNC.Exp, scale=-DECAY)
 
-        im2 = [piece_looked_up_plus_projection(3, piece) for piece in range(PIECES)]
-        last_factor = []
-        for piece in range(PIECES):
-            square = held.tile([P, PIECE], F32, name=f"square_im2_{piece}")
-            nc.vector.tensor_tensor(square[:], im2[piece][:], im2[piece][:], ALU.mult)
-            last = held.tile([P, PIECE], F32, name=f"last_factor{piece}")
-            nc.scalar.activation(last[:], square[:], FUNC.Exp, scale=-DECAY)
-            last_factor.append(last)
+        im2 = looked_up_plus_projection(3)
+        square = held.tile([P, N], F32, name="square_im2")
+        nc.vector.tensor_tensor(square[:], im2[:], im2[:], ALU.mult)
+        last_factor = held.tile([P, N], F32, name="last_factor")
+        nc.scalar.activation(last_factor[:], square[:], FUNC.Exp, scale=-DECAY)
         result = held.tile([P, 2, N], F32, name="result")
         nc.vector.scalar_tensor_tensor(result[:, 0, :], cos_less_1[:], 1.0, factor[:], ALU.add, ALU.mult)
         nc.vector.tensor_tensor(result[:, 1, :], sin_full[:], factor[:], ALU.mult)
-        out_halves = out.rearrange("(h p) j -> p h j", p=P)
-        for piece in range(PIECES):
-            columns = slice(piece * PIECE, (piece + 1) * PIECE)
-            nc.vector.tensor_tensor(
-                result[:, :, columns],
-                result[:, :, columns],
-                last_factor[piece][:].unsqueeze(1).to_broadcast([P, 2, PIECE]),
-                ALU.mult,
-            )
-            nc.sync.dma_start(out_halves[:, :, columns], result[:, :, columns])
+        nc.vector.tensor_tensor(
+            result[:], result[:], last_factor[:].unsqueeze(1).to_broadcast([P, 2, N]), ALU.mult
+        )
+        nc.sync.dma_start(out.rearrange("(h p) j -> p h j", p=P), result[:])

@@ -69,30 +69,31 @@ def tile_adaptivemultigabor2dlayer_kernel(tc, bias, w, x, offs, out):
         cos_half = held.tile([P, N], F32, name="cos_half")
         nc.scalar.activation(cos_half[:], minus_abs[:], FUNC.Sin, bias=quarter_turn[:], scale=PI_INSIDE)
 
-        im1 = looked_up_plus_projection(1)
+        trig = held.tile([P, 2, N], F32, name="trig")
         cos_less_1 = held.tile([P, N], F32, name="cos_less_1")
         nc.vector.scalar_tensor_tensor(cos_less_1[:], sin_half[:], -2.0, sin_half[:], ALU.mult, ALU.mult)
+        nc.vector.tensor_scalar(trig[:, 0, :], cos_less_1[:], 1.0, None, ALU.add)
+        nc.vector.scalar_tensor_tensor(trig[:, 1, :], sin_half[:], 2.0, cos_half[:], ALU.mult, ALU.mult)
+
+        im1 = looked_up_plus_projection(1)
         term = held.tile([P, N], F32, name="term")
         nc.vector.scalar_tensor_tensor(term[:], im1[:], OMEGA / DECAY, im1[:], ALU.add, ALU.mult)
-        sin_full = held.tile([P, N], F32, name="sin_full")
-        nc.vector.scalar_tensor_tensor(sin_full[:], sin_half[:], 2.0, cos_half[:], ALU.mult, ALU.mult)
         nc.vector.tensor_tensor(total[:], total[:], term[:], ALU.add)
 
         re2 = looked_up_plus_projection(2)
-        square = held.tile([P, N], F32, name="square_re2")
-        nc.vector.tensor_tensor(square[:], re2[:], re2[:], ALU.mult)
-        nc.vector.tensor_tensor(total[:], total[:], square[:], ALU.add)
+        square_re2 = held.tile([P, N], F32, name="square_re2")
+        nc.vector.tensor_tensor(square_re2[:], re2[:], re2[:], ALU.mult)
+        nc.vector.tensor_tensor(total[:], total[:], square_re2[:], ALU.add)
         factor = held.tile([P, N], F32, name="factor")
         nc.scalar.activation(factor[:], total[:], FUNC.Exp, scale=-DECAY)
 
         im2 = looked_up_plus_projection(3)
-        square = held.tile([P, N], F32, name="square_im2")
-        nc.vector.tensor_tensor(square[:], im2[:], im2[:], ALU.mult)
+        square_im2 = held.tile([P, N], F32, name="square_im2")
+        nc.vector.tensor_tensor(square_im2[:], im2[:], im2[:], ALU.mult)
         last_factor = held.tile([P, N], F32, name="last_factor")
-        nc.scalar.activation(last_factor[:], square[:], FUNC.Exp, scale=-DECAY)
+        nc.scalar.activation(last_factor[:], square_im2[:], FUNC.Exp, scale=-DECAY)
         result = held.tile([P, 2, N], F32, name="result")
-        nc.vector.scalar_tensor_tensor(result[:, 0, :], cos_less_1[:], 1.0, factor[:], ALU.add, ALU.mult)
-        nc.vector.tensor_tensor(result[:, 1, :], sin_full[:], factor[:], ALU.mult)
+        nc.vector.tensor_tensor(result[:], trig[:], factor[:].unsqueeze(1).to_broadcast([P, 2, N]), ALU.mult)
         nc.vector.tensor_tensor(
             result[:], result[:], last_factor[:].unsqueeze(1).to_broadcast([P, 2, N]), ALU.mult
         )

@@ -13,6 +13,7 @@ P = 128
 N = 256
 S = 2048
 BLOCKS = 4
+PIECES = 2
 
 FLOPS = 2 * P * (BLOCKS * P) * N
 
@@ -87,14 +88,29 @@ def tile_adaptivemultigabor2dlayer_kernel(tc, bias, w, x, offs, out):
         factor = held.tile([P, N], F32, name="factor")
         nc.scalar.activation(factor[:], total[:], FUNC.Exp, scale=-DECAY)
 
-        im2 = looked_up_plus_projection(3)
+        pieces = [slice(k * N // PIECES, (k + 1) * N // PIECES) for k in range(PIECES)]
+        im2 = held.tile([P, N], F32, name="im2")
         square_im2 = held.tile([P, N], F32, name="square_im2")
-        nc.vector.tensor_tensor(square_im2[:], im2[:], im2[:], ALU.mult)
         last_factor = held.tile([P, N], F32, name="last_factor")
-        nc.scalar.activation(last_factor[:], square_im2[:], FUNC.Exp, scale=-DECAY)
+        without_last = held.tile([P, 2, N], F32, name="without_last")
         result = held.tile([P, 2, N], F32, name="result")
-        nc.vector.tensor_tensor(result[:], trig[:], factor[:].unsqueeze(1).to_broadcast([P, 2, N]), ALU.mult)
-        nc.vector.tensor_tensor(
-            result[:], result[:], last_factor[:].unsqueeze(1).to_broadcast([P, 2, N]), ALU.mult
-        )
+        for piece in pieces:
+            nc.vector.tensor_tensor(
+                im2[:, piece],
+                windows[3][:].indirect(offsets[:, piece.start // 16 : piece.stop // 16]),
+                projections[3][:, piece],
+                ALU.add,
+            )
+        for piece in pieces:
+            nc.vector.tensor_tensor(square_im2[:, piece], im2[:, piece], im2[:, piece], ALU.mult)
+        for piece in pieces:
+            nc.scalar.activation(last_factor[:, piece], square_im2[:, piece], FUNC.Exp, scale=-DECAY)
+        nc.vector.tensor_tensor(without_last[:], trig[:], factor[:].unsqueeze(1).to_broadcast([P, 2, N]), ALU.mult)
+        for piece in pieces:
+            nc.vector.tensor_tensor(
+                result[:, :, piece],
+                without_last[:, :, piece],
+                last_factor[:, piece].unsqueeze(1).to_broadcast([P, 2, N // PIECES]),
+                ALU.mult,
+            )
         nc.sync.dma_start(out.rearrange("(h p) j -> p h j", p=P), result[:])

@@ -20,7 +20,7 @@ FLOPS = 2 * P * (BLOCKS * P) * N
 OMEGA = 30.0
 DECAY = 25.0
 TURNS = OMEGA / (2.0 * math.pi)
-PI_INSIDE = 3.1415925
+TWO_PI_INSIDE = 2.0 * 3.1415925
 
 
 def tile_adaptivemultigabor2dlayer_kernel(tc, bias, w, x, offs, out):
@@ -51,66 +51,57 @@ def tile_adaptivemultigabor2dlayer_kernel(tc, bias, w, x, offs, out):
             nc.vector.tensor_copy(proj[:], bank[:])
             projections.append(proj)
 
-        def looked_up_plus_projection(b):
-            lin = held.tile([P, N], F32, name=f"lin{b}")
-            nc.vector.tensor_tensor(lin[:], windows[b][:].indirect(offsets[:]), projections[b][:], ALU.add)
-            return lin
-
-        re1 = looked_up_plus_projection(0)
-        whole = held.tile([P, N], I32, name="whole")
-        nc.vector.tensor_scalar(whole[:], re1[:], TURNS, None, ALU.mult)
-        total = held.tile([P, N], F32, name="total")
-        nc.vector.tensor_tensor(total[:], re1[:], re1[:], ALU.mult)
-        part = held.tile([P, N], F32, name="part")
-        nc.vector.scalar_tensor_tensor(part[:], re1[:], TURNS, whole[:], ALU.mult, ALU.subtract)
-        sin_half = held.tile([P, N], F32, name="sin_half")
-        nc.scalar.activation(sin_half[:], part[:], FUNC.Sin, scale=PI_INSIDE)
-        minus_abs = held.tile([P, N], F32, name="minus_abs")
-        nc.vector.scalar_tensor_tensor(minus_abs[:], part[:], -1.0, part[:], ALU.mult, ALU.min)
-        cos_half = held.tile([P, N], F32, name="cos_half")
-        nc.scalar.activation(cos_half[:], minus_abs[:], FUNC.Sin, bias=quarter_turn[:], scale=PI_INSIDE)
-
-        trig = held.tile([P, 2, N], F32, name="trig")
-        cos_less_1 = held.tile([P, N], F32, name="cos_less_1")
-        nc.vector.scalar_tensor_tensor(cos_less_1[:], sin_half[:], -2.0, sin_half[:], ALU.mult, ALU.mult)
-        nc.vector.tensor_scalar(trig[:, 0, :], cos_less_1[:], 1.0, None, ALU.add)
-        nc.vector.scalar_tensor_tensor(trig[:, 1, :], sin_half[:], 2.0, cos_half[:], ALU.mult, ALU.mult)
-
-        im1 = looked_up_plus_projection(1)
-        term = held.tile([P, N], F32, name="term")
-        nc.vector.scalar_tensor_tensor(term[:], im1[:], OMEGA / DECAY, im1[:], ALU.add, ALU.mult)
-        nc.vector.tensor_tensor(total[:], total[:], term[:], ALU.add)
-
-        re2 = looked_up_plus_projection(2)
-        square_re2 = held.tile([P, N], F32, name="square_re2")
-        nc.vector.tensor_tensor(square_re2[:], re2[:], re2[:], ALU.mult)
-        nc.vector.tensor_tensor(total[:], total[:], square_re2[:], ALU.add)
-        factor = held.tile([P, N], F32, name="factor")
-        nc.scalar.activation(factor[:], total[:], FUNC.Exp, scale=-DECAY)
-
-        pieces = [slice(k * N // PIECES, (k + 1) * N // PIECES) for k in range(PIECES)]
-        im2 = held.tile([P, N], F32, name="im2")
-        square_im2 = held.tile([P, N], F32, name="square_im2")
-        last_factor = held.tile([P, N], F32, name="last_factor")
-        without_last = held.tile([P, 2, N], F32, name="without_last")
-        result = held.tile([P, 2, N], F32, name="result")
-        for piece in pieces:
+        def look_up_and_add(lin, b, piece):
             nc.vector.tensor_tensor(
-                im2[:, piece],
-                windows[3][:].indirect(offsets[:, piece.start // 16 : piece.stop // 16]),
-                projections[3][:, piece],
+                lin[:, piece],
+                windows[b][:].indirect(offsets[:, piece.start // 16 : piece.stop // 16]),
+                projections[b][:, piece],
                 ALU.add,
             )
-        for piece in pieces:
-            nc.vector.tensor_tensor(square_im2[:, piece], im2[:, piece], im2[:, piece], ALU.mult)
-        for piece in pieces:
-            nc.scalar.activation(last_factor[:, piece], square_im2[:, piece], FUNC.Exp, scale=-DECAY)
-        nc.vector.tensor_tensor(without_last[:], trig[:], factor[:].unsqueeze(1).to_broadcast([P, 2, N]), ALU.mult)
-        for piece in pieces:
-            nc.vector.tensor_tensor(
-                result[:, :, piece],
-                without_last[:, :, piece],
-                last_factor[:, piece].unsqueeze(1).to_broadcast([P, 2, N // PIECES]),
-                ALU.mult,
-            )
-        nc.sync.dma_start(out.rearrange("(h p) j -> p h j", p=P), result[:])
+
+        whole_list = slice(0, N)
+
+        re1 = held.tile([P, N], F32, name="re1")
+        look_up_and_add(re1, 0, whole_list)
+        whole = held.tile([P, N], I32, name="whole")
+        nc.vector.tensor_scalar(whole[:], re1[:], TURNS, None, ALU.mult)
+        part = held.tile([P, N], F32, name="part")
+        nc.vector.scalar_tensor_tensor(part[:], re1[:], TURNS, whole[:], ALU.mult, ALU.subtract)
+        trig = held.tile([P, 2, N], F32, name="trig")
+        nc.scalar.activation(trig[:, 1, :], part[:], FUNC.Sin, scale=TWO_PI_INSIDE)
+        minus_abs = held.tile([P, N], F32, name="minus_abs")
+        nc.vector.scalar_tensor_tensor(minus_abs[:], part[:], -1.0, part[:], ALU.mult, ALU.min)
+        nc.scalar.activation(trig[:, 0, :], minus_abs[:], FUNC.Sin, bias=quarter_turn[:], scale=TWO_PI_INSIDE)
+        square_re1 = held.tile([P, N], F32, name="square_re1")
+        nc.vector.tensor_tensor(square_re1[:], re1[:], re1[:], ALU.mult)
+
+        im1 = held.tile([P, N], F32, name="im1")
+        look_up_and_add(im1, 1, whole_list)
+        term = held.tile([P, N], F32, name="term")
+        nc.vector.scalar_tensor_tensor(term[:], im1[:], OMEGA / DECAY, im1[:], ALU.add, ALU.mult)
+        total = held.tile([P, N], F32, name="total")
+        nc.vector.tensor_tensor(total[:], square_re1[:], term[:], ALU.add)
+        factor = held.tile([P, N], F32, name="factor")
+        nc.scalar.activation(factor[:], total[:], FUNC.Exp, scale=-DECAY)
+        product = held.tile([P, 2, N], F32, name="product1")
+        nc.vector.tensor_tensor(product[:], trig[:], factor[:].unsqueeze(1).to_broadcast([P, 2, N]), ALU.mult)
+
+        pieces = [slice(k * N // PIECES, (k + 1) * N // PIECES) for k in range(PIECES)]
+        for b in (2, 3):
+            lin = held.tile([P, N], F32, name=f"lin{b}")
+            square = held.tile([P, N], F32, name=f"square{b}")
+            factor = held.tile([P, N], F32, name=f"factor{b}")
+            before = product
+            product = held.tile([P, 2, N], F32, name=f"product{b}")
+            for piece in pieces:
+                look_up_and_add(lin, b, piece)
+                nc.vector.tensor_tensor(square[:, piece], lin[:, piece], lin[:, piece], ALU.mult)
+                nc.scalar.activation(factor[:, piece], square[:, piece], FUNC.Exp, scale=-DECAY)
+            for piece in pieces:
+                nc.vector.tensor_tensor(
+                    product[:, :, piece],
+                    before[:, :, piece],
+                    factor[:, piece].unsqueeze(1).to_broadcast([P, 2, N // PIECES]),
+                    ALU.mult,
+                )
+        nc.sync.dma_start(out.rearrange("(h p) j -> p h j", p=P), product[:])

@@ -95,8 +95,8 @@ def tile_adaptivemultigabor2dlayer_kernel(tc, bias, w, x, offs, out):
             product = held.tile([P, 2, N], F32, name=f"product{b}")
             for piece in pieces:
                 look_up_and_add(lin, b, piece)
-                nc.vector.tensor_tensor(square[:, piece], lin[:, piece], lin[:, piece], ALU.mult)
-                nc.scalar.activation(factor[:, piece], square[:, piece], FUNC.Exp, scale=-DECAY)
+                nc.scalar.activation(square[:, piece], lin[:, piece], FUNC.Square, scale=math.sqrt(DECAY))
+                nc.scalar.activation(factor[:, piece], square[:, piece], FUNC.Exp, scale=-1.0)
             for piece in pieces:
                 nc.vector.tensor_tensor(
                     product[:, :, piece],

@@ -41,7 +41,7 @@ def tile_adaptivemultigabor2dlayer_kernel(tc, bias, w, x, offs, out):
             nc.sync.dma_start(window[:], bias[b * P : (b + 1) * P, :])
             windows.append(window)
         quarter_turn = held.tile([P, 1], F32, name="quarter_turn")
-        nc.gpsimd.memset(quarter_turn[:], math.pi / 2.0)
+        nc.vector.memset(quarter_turn[:], math.pi / 2.0)
 
         projections = []
         for b in range(BLOCKS):

@@ -5,7 +5,6 @@ import concourse.mybir as mybir
 F32 = mybir.dt.float32
 BF16 = mybir.dt.bfloat16
 U16 = mybir.dt.uint16
-I32 = mybir.dt.int32
 ALU = mybir.AluOpType
 FUNC = mybir.ActivationFunctionType
 
@@ -19,8 +18,6 @@ FLOPS = 2 * P * (BLOCKS * P) * N
 
 OMEGA = 30.0
 DECAY = 25.0
-TURNS = OMEGA / (2.0 * math.pi)
-TWO_PI_INSIDE = 2.0 * 3.1415925
 
 
 def tile_adaptivemultigabor2dlayer_kernel(tc, bias, w, x, offs, out):
@@ -63,15 +60,11 @@ def tile_adaptivemultigabor2dlayer_kernel(tc, bias, w, x, offs, out):
 
         re1 = held.tile([P, N], F32, name="re1")
         look_up_and_add(re1, 0, whole_list)
-        whole = held.tile([P, N], I32, name="whole")
-        nc.vector.tensor_scalar(whole[:], re1[:], TURNS, None, ALU.mult)
-        part = held.tile([P, N], F32, name="part")
-        nc.vector.scalar_tensor_tensor(part[:], re1[:], TURNS, whole[:], ALU.mult, ALU.subtract)
         trig = held.tile([P, 2, N], F32, name="trig")
-        nc.scalar.activation(trig[:, 1, :], part[:], FUNC.Sin, scale=TWO_PI_INSIDE)
-        minus_abs = held.tile([P, N], F32, name="minus_abs")
-        nc.vector.scalar_tensor_tensor(minus_abs[:], part[:], -1.0, part[:], ALU.mult, ALU.min)
-        nc.scalar.activation(trig[:, 0, :], minus_abs[:], FUNC.Sin, bias=quarter_turn[:], scale=TWO_PI_INSIDE)
+        nc.scalar.activation(trig[:, 1, :], re1[:], FUNC.Sin, scale=OMEGA)
+        abs_re1 = held.tile([P, N], F32, name="abs_re1")
+        nc.scalar.activation(abs_re1[:], re1[:], FUNC.Abs)
+        nc.scalar.activation(trig[:, 0, :], abs_re1[:], FUNC.Sin, bias=quarter_turn[:], scale=-OMEGA)
         square_re1 = held.tile([P, N], F32, name="square_re1")
         nc.vector.tensor_tensor(square_re1[:], re1[:], re1[:], ALU.mult)
 

@@ -56,30 +56,34 @@ def tile_adaptivemultigabor2dlayer_kernel(tc, bias, w, x, offs, out):
                 ALU.add,
             )
 
-        whole_list = slice(0, N)
+        pieces = [slice(k * N // PIECES, (k + 1) * N // PIECES) for k in range(PIECES)]
+
+        def both_parts(tile, piece):
+            return tile[:, piece].unsqueeze(1).to_broadcast([P, 2, N // PIECES])
 
         re1 = held.tile([P, N], F32, name="re1")
-        look_up_and_add(re1, 0, whole_list)
-        trig = held.tile([P, 2, N], F32, name="trig")
-        nc.scalar.activation(trig[:, 1, :], re1[:], FUNC.Sin, scale=OMEGA)
         abs_re1 = held.tile([P, N], F32, name="abs_re1")
-        nc.scalar.activation(abs_re1[:], re1[:], FUNC.Abs)
-        nc.scalar.activation(trig[:, 0, :], abs_re1[:], FUNC.Sin, bias=quarter_turn[:], scale=-OMEGA)
+        trig = held.tile([P, 2, N], F32, name="trig")
         square_re1 = held.tile([P, N], F32, name="square_re1")
-        nc.vector.tensor_tensor(square_re1[:], re1[:], re1[:], ALU.mult)
+        for piece in pieces:
+            look_up_and_add(re1, 0, piece)
+            nc.scalar.activation(trig[:, 1, piece], re1[:, piece], FUNC.Sin, scale=OMEGA)
+            nc.scalar.activation(abs_re1[:, piece], re1[:, piece], FUNC.Abs)
+            nc.scalar.activation(trig[:, 0, piece], abs_re1[:, piece], FUNC.Sin, bias=quarter_turn[:], scale=-OMEGA)
+            nc.vector.tensor_tensor(square_re1[:, piece], re1[:, piece], re1[:, piece], ALU.mult)
 
         im1 = held.tile([P, N], F32, name="im1")
-        look_up_and_add(im1, 1, whole_list)
         term = held.tile([P, N], F32, name="term")
-        nc.vector.scalar_tensor_tensor(term[:], im1[:], OMEGA / DECAY, im1[:], ALU.add, ALU.mult)
         total = held.tile([P, N], F32, name="total")
-        nc.vector.tensor_tensor(total[:], square_re1[:], term[:], ALU.add)
-        factor = held.tile([P, N], F32, name="factor")
-        nc.scalar.activation(factor[:], total[:], FUNC.Exp, scale=-DECAY)
+        factor = held.tile([P, N], F32, name="factor1")
         product = held.tile([P, 2, N], F32, name="product1")
-        nc.vector.tensor_tensor(product[:], trig[:], factor[:].unsqueeze(1).to_broadcast([P, 2, N]), ALU.mult)
+        for piece in pieces:
+            look_up_and_add(im1, 1, piece)
+            nc.vector.scalar_tensor_tensor(term[:, piece], im1[:, piece], OMEGA / DECAY, im1[:, piece], ALU.add, ALU.mult)
+            nc.vector.tensor_tensor(total[:, piece], square_re1[:, piece], term[:, piece], ALU.add)
+            nc.scalar.activation(factor[:, piece], total[:, piece], FUNC.Exp, scale=-DECAY)
+            nc.vector.tensor_tensor(product[:, :, piece], trig[:, :, piece], both_parts(factor, piece), ALU.mult)
 
-        pieces = [slice(k * N // PIECES, (k + 1) * N // PIECES) for k in range(PIECES)]
         for b in (2, 3):
             lin = held.tile([P, N], F32, name=f"lin{b}")
             square = held.tile([P, N], F32, name=f"square{b}")
@@ -91,10 +95,5 @@ def tile_adaptivemultigabor2dlayer_kernel(tc, bias, w, x, offs, out):
                 nc.scalar.activation(square[:, piece], lin[:, piece], FUNC.Square, scale=math.sqrt(DECAY))
                 nc.scalar.activation(factor[:, piece], square[:, piece], FUNC.Exp, scale=-1.0)
             for piece in pieces:
-                nc.vector.tensor_tensor(
-                    product[:, :, piece],
-                    before[:, :, piece],
-                    factor[:, piece].unsqueeze(1).to_broadcast([P, 2, N // PIECES]),
-                    ALU.mult,
-                )
+                nc.vector.tensor_tensor(product[:, :, piece], before[:, :, piece], both_parts(factor, piece), ALU.mult)
         nc.sync.dma_start(out.rearrange("(h p) j -> p h j", p=P), product[:])

@@ -12,6 +12,7 @@ P = 128
 N = 256
 S = 2048
 BLOCKS = 4
+ROW_ALIGN = 256
 PIECES = 2
 
 FLOPS = 2 * P * (BLOCKS * P) * N
@@ -26,15 +27,15 @@ def tile_adaptivemultigabor2dlayer_kernel(tc, bias, w, x, offs, out):
         tc.tile_pool(name="held", bufs=1) as held,
         tc.psum_pool(name="psum", bufs=1) as psum,
     ):
-        offsets = held.tile([P, N // 16], U16, name="offsets")
+        offsets = held.tile([P, N // 16], U16, name="offsets", align_bytes=ROW_ALIGN)
         nc.sync.dma_start(offsets[:], offs)
-        x_sb = held.tile([P, N], BF16, name="x_sb")
+        x_sb = held.tile([P, N], BF16, name="x_sb", align_bytes=ROW_ALIGN)
         nc.sync.dma_start(x_sb[:], x)
-        w_sb = held.tile([P, BLOCKS * P], BF16, name="w_sb")
+        w_sb = held.tile([P, BLOCKS * P], BF16, name="w_sb", align_bytes=ROW_ALIGN)
         nc.sync.dma_start(w_sb[:], w)
         windows = []
         for b in range(BLOCKS):
-            window = held.tile([P, S], F32, name=f"window{b}")
+            window = held.tile([P, S], F32, name=f"window{b}", align_bytes=ROW_ALIGN)
             nc.sync.dma_start(window[:], bias[b * P : (b + 1) * P, :])
             windows.append(window)
         quarter_turn = held.tile([P, 1], F32, name="quarter_turn")
@@ -89,7 +90,7 @@ def tile_adaptivemultigabor2dlayer_kernel(tc, bias, w, x, offs, out):
             square = held.tile([P, N], F32, name=f"square{b}")
             factor = held.tile([P, N], F32, name=f"factor{b}")
             before = product
-            product = held.tile([P, 2, N], F32, name=f"product{b}")
+            product = held.tile([P, 2, N], F32, name=f"product{b}", align_bytes=ROW_ALIGN)
             for piece in pieces:
                 look_up_and_add(lin, b, piece)
                 nc.scalar.activation(square[:, piece], lin[:, piece], FUNC.Square, scale=math.sqrt(DECAY))

@@ -27,17 +27,16 @@ def tile_adaptivemultigabor2dlayer_kernel(tc, bias, w, x, offs, out):
         tc.tile_pool(name="held", bufs=1) as held,
         tc.psum_pool(name="psum", bufs=1) as psum,
     ):
-        offsets = held.tile([P, N // 16], U16, name="offsets", align_bytes=ROW_ALIGN)
-        nc.sync.dma_start(offsets[:], offs)
-        x_sb = held.tile([P, N], BF16, name="x_sb", align_bytes=ROW_ALIGN)
-        nc.sync.dma_start(x_sb[:], x)
         w_sb = held.tile([P, BLOCKS * P], BF16, name="w_sb", align_bytes=ROW_ALIGN)
         nc.sync.dma_start(w_sb[:], w)
-        windows = []
-        for b in range(BLOCKS):
-            window = held.tile([P, S], F32, name=f"window{b}", align_bytes=ROW_ALIGN)
-            nc.sync.dma_start(window[:], bias[b * P : (b + 1) * P, :])
-            windows.append(window)
+        x_sb = held.tile([P, N], BF16, name="x_sb", align_bytes=ROW_ALIGN)
+        nc.sync.dma_start(x_sb[:], x)
+        windows = [held.tile([P, S], F32, name=f"window{b}", align_bytes=ROW_ALIGN) for b in range(BLOCKS)]
+        offsets = held.tile([P, N // 16], U16, name="offsets", align_bytes=ROW_ALIGN)
+        nc.sync.dma_start(windows[0][:], bias[:P, :])
+        nc.sync.dma_start(offsets[:], offs)
+        for b in range(1, BLOCKS):
+            nc.sync.dma_start(windows[b][:], bias[b * P : (b + 1) * P, :])
         quarter_turn = held.tile([P, 1], F32, name="quarter_turn")
         nc.vector.memset(quarter_turn[:], math.pi / 2.0)
 

@@ -92,8 +92,12 @@ def tile_adaptivemultigabor2dlayer_kernel(tc, bias, w, x, offs, out):
             product = held.tile([P, 2, N], F32, name=f"product{b}", align_bytes=ROW_ALIGN)
             for piece in pieces:
                 look_up_and_add(lin, b, piece)
-                nc.scalar.activation(square[:, piece], lin[:, piece], FUNC.Square, scale=math.sqrt(DECAY))
-                nc.scalar.activation(factor[:, piece], square[:, piece], FUNC.Exp, scale=-1.0)
+                if b == BLOCKS - 1 and piece is pieces[-1]:
+                    nc.vector.tensor_tensor(square[:, piece], lin[:, piece], lin[:, piece], ALU.mult)
+                    nc.scalar.activation(factor[:, piece], square[:, piece], FUNC.Exp, scale=-DECAY)
+                else:
+                    nc.scalar.activation(square[:, piece], lin[:, piece], FUNC.Square, scale=math.sqrt(DECAY))
+                    nc.scalar.activation(factor[:, piece], square[:, piece], FUNC.Exp, scale=-1.0)
             for piece in pieces:
                 nc.vector.tensor_tensor(product[:, :, piece], before[:, :, piece], both_parts(factor, piece), ALU.mult)
         nc.sync.dma_start(out.rearrange("(h p) j -> p h j", p=P), product[:])

@@ -58,8 +58,10 @@ def tile_adaptivemultigabor2dlayer_kernel(tc, bias, w, x, offs, out):
 
         pieces = [slice(k * N // PIECES, (k + 1) * N // PIECES) for k in range(PIECES)]
 
+        last_pieces = [slice(0, 96), slice(96, 192), slice(192, N)]
+
         def both_parts(tile, piece):
-            return tile[:, piece].unsqueeze(1).to_broadcast([P, 2, N // PIECES])
+            return tile[:, piece].unsqueeze(1).to_broadcast([P, 2, piece.stop - piece.start])
 
         re1 = held.tile([P, N], F32, name="re1")
         abs_re1 = held.tile([P, N], F32, name="abs_re1")
@@ -84,20 +86,19 @@ def tile_adaptivemultigabor2dlayer_kernel(tc, bias, w, x, offs, out):
             nc.scalar.activation(factor[:, piece], total[:, piece], FUNC.Exp, scale=-DECAY)
             nc.vector.tensor_tensor(product[:, :, piece], trig[:, :, piece], both_parts(factor, piece), ALU.mult)
 
-        for b in (2, 3):
+        for b, cut in ((2, pieces), (3, last_pieces)):
             lin = held.tile([P, N], F32, name=f"lin{b}")
             square = held.tile([P, N], F32, name=f"square{b}")
             factor = held.tile([P, N], F32, name=f"factor{b}")
             before = product
             product = held.tile([P, 2, N], F32, name=f"product{b}", align_bytes=ROW_ALIGN)
-            for piece in pieces:
+            for piece in cut:
                 look_up_and_add(lin, b, piece)
-                if b == BLOCKS - 1 and piece is pieces[-1]:
-                    nc.vector.tensor_tensor(square[:, piece], lin[:, piece], lin[:, piece], ALU.mult)
-                    nc.scalar.activation(factor[:, piece], square[:, piece], FUNC.Exp, scale=-DECAY)
+                if b == 2 or piece.start == 0:
+                    nc.scalar.activation(square[:, piece], lin[:, piece], FUNC.Square)
                 else:
-                    nc.scalar.activation(square[:, piece], lin[:, piece], FUNC.Square, scale=math.sqrt(DECAY))
-                    nc.scalar.activation(factor[:, piece], square[:, piece], FUNC.Exp, scale=-1.0)
-            for piece in pieces:
+                    nc.vector.tensor_tensor(square[:, piece], lin[:, piece], lin[:, piece], ALU.mult)
+                nc.scalar.activation(factor[:, piece], square[:, piece], FUNC.Exp, scale=-DECAY)
+            for piece in cut:
                 nc.vector.tensor_tensor(product[:, :, piece], before[:, :, piece], both_parts(factor, piece), ALU.mult)
         nc.sync.dma_start(out.rearrange("(h p) j -> p h j", p=P), product[:])

@@ -58,7 +58,7 @@ def tile_adaptivemultigabor2dlayer_kernel(tc, bias, w, x, offs, out):
 
         pieces = [slice(k * N // PIECES, (k + 1) * N // PIECES) for k in range(PIECES)]
 
-        last_pieces = [slice(0, 96), slice(96, 192), slice(192, N)]
+        last_pieces = [slice(k * N // (2 * PIECES), (k + 1) * N // (2 * PIECES)) for k in range(2 * PIECES)]
 
         def both_parts(tile, piece):
             return tile[:, piece].unsqueeze(1).to_broadcast([P, 2, piece.stop - piece.start])
@@ -94,7 +94,7 @@ def tile_adaptivemultigabor2dlayer_kernel(tc, bias, w, x, offs, out):
             product = held.tile([P, 2, N], F32, name=f"product{b}", align_bytes=ROW_ALIGN)
             for piece in cut:
                 look_up_and_add(lin, b, piece)
-                if b == 2 or piece.start == 0:
+                if b == 2 or piece.start < N // 2:
                     nc.scalar.activation(square[:, piece], lin[:, piece], FUNC.Square)
                 else:
                     nc.vector.tensor_tensor(square[:, piece], lin[:, piece], lin[:, piece], ALU.mult)

@@ -31,7 +31,10 @@ def tile_adaptivemultigabor2dlayer_kernel(tc, bias, w, x, offs, out):
         nc.sync.dma_start(w_sb[:], w)
         x_sb = held.tile([P, N], BF16, name="x_sb", align_bytes=ROW_ALIGN)
         nc.sync.dma_start(x_sb[:], x)
-        windows = [held.tile([P, S], F32, name=f"window{b}", align_bytes=ROW_ALIGN) for b in range(BLOCKS)]
+        windows = [
+            held.tile([P, S], F32, name=f"window{b}", tag="window", bufs=BLOCKS - 1, align_bytes=ROW_ALIGN)
+            for b in range(BLOCKS)
+        ]
         offsets = held.tile([P, N // 16], U16, name="offsets", align_bytes=ROW_ALIGN)
         nc.sync.dma_start(windows[0][:], bias[:P, :])
         nc.sync.dma_start(offsets[:], offs)

@@ -5,6 +5,7 @@ import concourse.mybir as mybir
 F32 = mybir.dt.float32
 BF16 = mybir.dt.bfloat16
 U16 = mybir.dt.uint16
+I32 = mybir.dt.int32
 ALU = mybir.AluOpType
 FUNC = mybir.ActivationFunctionType
 
@@ -18,6 +19,7 @@ PIECES = 2
 FLOPS = 2 * P * (BLOCKS * P) * N
 
 OMEGA = 30.0
+TURN = 2.0 * math.pi
 DECAY = 25.0
 
 
@@ -41,7 +43,7 @@ def tile_adaptivemultigabor2dlayer_kernel(tc, bias, w, x, offs, out):
         for b in range(1, BLOCKS):
             nc.sync.dma_start(windows[b][:], bias[b * P : (b + 1) * P, :])
         quarter_turn = held.tile([P, 1], F32, name="quarter_turn")
-        nc.vector.memset(quarter_turn[:], math.pi / 2.0)
+        nc.vector.memset(quarter_turn[:], TURN / 4.0)
 
         projections = []
         for b in range(BLOCKS):
@@ -67,14 +69,18 @@ def tile_adaptivemultigabor2dlayer_kernel(tc, bias, w, x, offs, out):
             return tile[:, piece].unsqueeze(1).to_broadcast([P, 2, piece.stop - piece.start])
 
         re1 = held.tile([P, N], F32, name="re1")
-        abs_re1 = held.tile([P, N], F32, name="abs_re1")
+        turns = held.tile([P, N], I32, name="turns")
+        part = held.tile([P, N], F32, name="part")
+        abs_part = held.tile([P, N], F32, name="abs_part")
         trig = held.tile([P, 2, N], F32, name="trig")
         square_re1 = held.tile([P, N], F32, name="square_re1")
         for piece in pieces:
             look_up_and_add(re1, 0, piece)
-            nc.scalar.activation(trig[:, 1, piece], re1[:, piece], FUNC.Sin, scale=OMEGA)
-            nc.scalar.activation(abs_re1[:, piece], re1[:, piece], FUNC.Abs)
-            nc.scalar.activation(trig[:, 0, piece], abs_re1[:, piece], FUNC.Sin, bias=quarter_turn[:], scale=-OMEGA)
+            nc.vector.tensor_scalar_mul(turns[:, piece], re1[:, piece], OMEGA / TURN)
+            nc.vector.scalar_tensor_tensor(part[:, piece], re1[:, piece], OMEGA / TURN, turns[:, piece], ALU.mult, ALU.subtract)
+            nc.scalar.activation(trig[:, 1, piece], part[:, piece], FUNC.Sin, scale=TURN)
+            nc.scalar.activation(abs_part[:, piece], part[:, piece], FUNC.Abs)
+            nc.scalar.activation(trig[:, 0, piece], abs_part[:, piece], FUNC.Sin, bias=quarter_turn[:], scale=-TURN)
             nc.vector.tensor_tensor(square_re1[:, piece], re1[:, piece], re1[:, piece], ALU.mult)
 
         im1 = held.tile([P, N], F32, name="im1")

@@ -29,27 +29,30 @@ def tile_adaptivemultigabor2dlayer_kernel(tc, bias, w, x, offs, out):
         tc.tile_pool(name="held", bufs=1) as held,
         tc.psum_pool(name="psum", bufs=1) as psum,
     ):
-        w_sb = held.tile([P, BLOCKS * P], BF16, name="w_sb", align_bytes=ROW_ALIGN)
+        def sbuf(shape, dtype, **kwargs):
+            return held.tile(shape, dtype, align_bytes=ROW_ALIGN, **kwargs)
+
+        w_sb = sbuf([P, BLOCKS * P], BF16, name="w_sb")
         nc.sync.dma_start(w_sb[:], w)
-        x_sb = held.tile([P, N], BF16, name="x_sb", align_bytes=ROW_ALIGN)
+        x_sb = sbuf([P, N], BF16, name="x_sb")
         nc.sync.dma_start(x_sb[:], x)
         windows = [
-            held.tile([P, S], F32, name=f"window{b}", tag="window", bufs=BLOCKS - 1, align_bytes=ROW_ALIGN)
+            sbuf([P, S], F32, name=f"window{b}", tag="window", bufs=BLOCKS - 1)
             for b in range(BLOCKS)
         ]
-        offsets = held.tile([P, N // 16], U16, name="offsets", align_bytes=ROW_ALIGN)
+        offsets = sbuf([P, N // 16], U16, name="offsets")
         nc.sync.dma_start(windows[0][:], bias[:P, :])
         nc.sync.dma_start(offsets[:], offs)
         for b in range(1, BLOCKS):
             nc.sync.dma_start(windows[b][:], bias[b * P : (b + 1) * P, :])
-        quarter_turn = held.tile([P, 1], F32, name="quarter_turn")
+        quarter_turn = sbuf([P, 1], F32, name="quarter_turn")
         nc.vector.memset(quarter_turn[:], TURN / 4.0)
 
         projections = []
         for b in range(BLOCKS):
             bank = psum.tile([P, N], F32, name=f"bank{b}")
             nc.tensor.matmul(bank[:], w_sb[:, b * P : (b + 1) * P], x_sb[:], start=True, stop=True)
-            proj = held.tile([P, N], F32, name=f"proj{b}")
+            proj = sbuf([P, N], F32, name=f"proj{b}")
             nc.vector.tensor_copy(proj[:], bank[:])
             projections.append(proj)
 
@@ -68,12 +71,12 @@ def tile_adaptivemultigabor2dlayer_kernel(tc, bias, w, x, offs, out):
         def both_parts(tile, piece):
             return tile[:, piece].unsqueeze(1).to_broadcast([P, 2, piece.stop - piece.start])
 
-        re1 = held.tile([P, N], F32, name="re1")
-        turns = held.tile([P, N], I32, name="turns")
-        part = held.tile([P, N], F32, name="part")
-        abs_part = held.tile([P, N], F32, name="abs_part")
-        trig = held.tile([P, 2, N], F32, name="trig")
-        square_re1 = held.tile([P, N], F32, name="square_re1")
+        re1 = sbuf([P, N], F32, name="re1")
+        turns = sbuf([P, N], I32, name="turns")
+        part = sbuf([P, N], F32, name="part")
+        abs_part = sbuf([P, N], F32, name="abs_part")
+        trig = sbuf([P, 2, N], F32, name="trig")
+        square_re1 = sbuf([P, N], F32, name="square_re1")
         for piece in pieces:
             look_up_and_add(re1, 0, piece)
             nc.vector.tensor_scalar_mul(turns[:, piece], re1[:, piece], OMEGA / TURN)
@@ -83,11 +86,11 @@ def tile_adaptivemultigabor2dlayer_kernel(tc, bias, w, x, offs, out):
             nc.scalar.activation(trig[:, 0, piece], abs_part[:, piece], FUNC.Sin, bias=quarter_turn[:], scale=-TURN)
             nc.vector.tensor_tensor(square_re1[:, piece], re1[:, piece], re1[:, piece], ALU.mult)
 
-        im1 = held.tile([P, N], F32, name="im1")
-        term = held.tile([P, N], F32, name="term")
-        total = held.tile([P, N], F32, name="total")
-        factor = held.tile([P, N], F32, name="factor1")
-        product = held.tile([P, 2, N], F32, name="product1")
+        im1 = sbuf([P, N], F32, name="im1")
+        term = sbuf([P, N], F32, name="term")
+        total = sbuf([P, N], F32, name="total")
+        factor = sbuf([P, N], F32, name="factor1")
+        product = sbuf([P, 2, N], F32, name="product1")
         for piece in pieces:
             look_up_and_add(im1, 1, piece)
             nc.vector.scalar_tensor_tensor(term[:, piece], im1[:, piece], OMEGA / DECAY, im1[:, piece], ALU.add, ALU.mult)
@@ -96,11 +99,11 @@ def tile_adaptivemultigabor2dlayer_kernel(tc, bias, w, x, offs, out):
             nc.vector.tensor_tensor(product[:, :, piece], trig[:, :, piece], both_parts(factor, piece), ALU.mult)
 
         for b, cut in ((2, pieces), (3, last_pieces)):
-            lin = held.tile([P, N], F32, name=f"lin{b}")
-            square = held.tile([P, N], F32, name=f"square{b}")
-            factor = held.tile([P, N], F32, name=f"factor{b}")
+            lin = sbuf([P, N], F32, name=f"lin{b}")
+            square = sbuf([P, N], F32, name=f"square{b}")
+            factor = sbuf([P, N], F32, name=f"factor{b}")
             before = product
-            product = held.tile([P, 2, N], F32, name=f"product{b}", align_bytes=ROW_ALIGN)
+            product = sbuf([P, 2, N], F32, name=f"product{b}")
             for piece in cut:
                 look_up_and_add(lin, b, piece)
                 if b == 2 or piece.start < N // 2:

import math

import concourse.mybir as mybir

F32 = mybir.dt.float32
BF16 = mybir.dt.bfloat16
U16 = mybir.dt.uint16
I32 = mybir.dt.int32
ALU = mybir.AluOpType
FUNC = mybir.ActivationFunctionType

P = 128
N = 256
S = 2048
BLOCKS = 4
ROW_ALIGN = 256
PIECES = 2

FLOPS = 2 * P * (BLOCKS * P) * N

OMEGA = 30.0
TURN = 2.0 * math.pi
DECAY = 25.0


def tile_adaptivemultigabor2dlayer_kernel(tc, bias, w, x, offs, out):
    nc = tc.nc
    with (
        tc.tile_pool(name="held", bufs=1) as held,
        tc.psum_pool(name="psum", bufs=1) as psum,
    ):
        def sbuf(shape, dtype, **kwargs):
            return held.tile(shape, dtype, align_bytes=ROW_ALIGN, **kwargs)

        w_sb = sbuf([P, BLOCKS * P], BF16, name="w_sb")
        nc.sync.dma_start(w_sb[:], w)
        x_sb = sbuf([P, N], BF16, name="x_sb")
        nc.sync.dma_start(x_sb[:], x)
        windows = [
            sbuf([P, S], F32, name=f"window{b}", tag="window", bufs=BLOCKS - 1)
            for b in range(BLOCKS)
        ]
        offsets = sbuf([P, N // 16], U16, name="offsets")
        nc.sync.dma_start(windows[0][:], bias[:P, :])
        nc.sync.dma_start(offsets[:], offs)
        for b in range(1, BLOCKS):
            nc.sync.dma_start(windows[b][:], bias[b * P : (b + 1) * P, :])
        quarter_turn = sbuf([P, 1], F32, name="quarter_turn")
        nc.vector.memset(quarter_turn[:], TURN / 4.0)

        projections = []
        for b in range(BLOCKS):
            bank = psum.tile([P, N], F32, name=f"bank{b}")
            nc.tensor.matmul(bank[:], w_sb[:, b * P : (b + 1) * P], x_sb[:], start=True, stop=True)
            proj = sbuf([P, N], F32, name=f"proj{b}")
            nc.vector.tensor_copy(proj[:], bank[:])
            projections.append(proj)

        def look_up_and_add(lin, b, piece):
            nc.vector.tensor_tensor(
                lin[:, piece],
                windows[b][:].indirect(offsets[:, piece.start // 16 : piece.stop // 16]),
                projections[b][:, piece],
                ALU.add,
            )

        pieces = [slice(k * N // PIECES, (k + 1) * N // PIECES) for k in range(PIECES)]

        last_pieces = [slice(k * N // (2 * PIECES), (k + 1) * N // (2 * PIECES)) for k in range(2 * PIECES)]

        def both_parts(tile, piece):
            return tile[:, piece].unsqueeze(1).to_broadcast([P, 2, piece.stop - piece.start])

        re1 = sbuf([P, N], F32, name="re1")
        turns = sbuf([P, N], I32, name="turns")
        part = sbuf([P, N], F32, name="part")
        abs_part = sbuf([P, N], F32, name="abs_part")
        trig = sbuf([P, 2, N], F32, name="trig")
        square_re1 = sbuf([P, N], F32, name="square_re1")
        for piece in pieces:
            look_up_and_add(re1, 0, piece)
            nc.vector.tensor_scalar_mul(turns[:, piece], re1[:, piece], OMEGA / TURN)
            nc.vector.scalar_tensor_tensor(part[:, piece], re1[:, piece], OMEGA / TURN, turns[:, piece], ALU.mult, ALU.subtract)
            nc.scalar.activation(trig[:, 1, piece], part[:, piece], FUNC.Sin, scale=TURN)
            nc.scalar.activation(abs_part[:, piece], part[:, piece], FUNC.Abs)
            nc.scalar.activation(trig[:, 0, piece], abs_part[:, piece], FUNC.Sin, bias=quarter_turn[:], scale=-TURN)
            nc.vector.tensor_tensor(square_re1[:, piece], re1[:, piece], re1[:, piece], ALU.mult)

        im1 = sbuf([P, N], F32, name="im1")
        term = sbuf([P, N], F32, name="term")
        total = sbuf([P, N], F32, name="total")
        factor = sbuf([P, N], F32, name="factor1")
        product = sbuf([P, 2, N], F32, name="product1")
        for piece in pieces:
            look_up_and_add(im1, 1, piece)
            nc.vector.scalar_tensor_tensor(term[:, piece], im1[:, piece], OMEGA / DECAY, im1[:, piece], ALU.add, ALU.mult)
            nc.vector.tensor_tensor(total[:, piece], square_re1[:, piece], term[:, piece], ALU.add)
            nc.scalar.activation(factor[:, piece], total[:, piece], FUNC.Exp, scale=-DECAY)
            nc.vector.tensor_tensor(product[:, :, piece], trig[:, :, piece], both_parts(factor, piece), ALU.mult)

        for b, cut in ((2, pieces), (3, last_pieces)):
            lin = sbuf([P, N], F32, name=f"lin{b}")
            square = sbuf([P, N], F32, name=f"square{b}")
            factor = sbuf([P, N], F32, name=f"factor{b}")
            before = product
            product = sbuf([P, 2, N], F32, name=f"product{b}")
            for piece in cut:
                look_up_and_add(lin, b, piece)
                if b == 2 or piece.start < N // 2:
                    nc.scalar.activation(square[:, piece], lin[:, piece], FUNC.Square)
                else:
                    nc.vector.tensor_tensor(square[:, piece], lin[:, piece], lin[:, piece], ALU.mult)
                nc.scalar.activation(factor[:, piece], square[:, piece], FUNC.Exp, scale=-DECAY)
            for piece in cut:
                nc.vector.tensor_tensor(product[:, :, piece], before[:, :, piece], both_parts(factor, piece), ALU.mult)
        nc.sync.dma_start(out.rearrange("(h p) j -> p h j", p=P), product[:])
